import numpy as np
import ml_dtypes


def mxq(x, axis, fmt="e4m3"):
    dtype, down = {"e4m3": (ml_dtypes.float8_e4m3fn, 7), "e5m2": (ml_dtypes.float8_e5m2, 14)}[fmt]
    v = np.moveaxis(np.asarray(x, np.float32).astype(ml_dtypes.bfloat16).astype(np.float64), axis, -1)
    blocks = v.reshape(v.shape[:-1] + (-1, 32))
    amax = np.abs(blocks).max(-1, keepdims=True)
    byte = np.maximum(np.where(amax > 0, np.frexp(amax)[1] - 1 + 127, 0) - down, 1)
    scale = np.exp2(byte - 127.0)
    codes = (blocks / scale).astype(np.float32).astype(dtype).astype(np.float64)
    return np.moveaxis((codes * scale).reshape(v.shape), -1, axis)


WIDE = False


def mx_kscale(k):
    if not WIDE:
        return np.ones(k)
    levels = np.array([10, -10, 5, -5, 0])
    a = np.random.permutation(np.resize(levels, k // 512 * 4)).reshape(k // 512, 4)
    idx = np.arange(k)
    return np.exp2(a[idx // 512, idx % 128 // 32])


BF16 = ml_dtypes.bfloat16


def bf(x):
    return np.asarray(x, np.float32).astype(BF16)


def f64(x):
    return np.asarray(x).astype(np.float64)


B, S, NS, DS, H = 4, 1024, 4, 128, 512
D = NS * DS


def setup_inputs():
    t, u = mx_kscale(H), mx_kscale(D)
    return {"hid": bf(0.6 * np.random.standard_normal((B, S, NS, H)) * t),
            "Wd": bf(1.5 * np.random.standard_normal((NS, H, DS)) / np.sqrt(H) / t[None, :, None] * u.reshape(NS, 1, DS)),
            "Wo": bf(np.random.standard_normal((D, D)) / np.sqrt(D) / u[:, None]),
            "x": bf(np.random.standard_normal((B, S, D)))}


def reference(hid, Wd, Wo, x):
    hq = mxq(f64(hid).transpose(0, 2, 1, 3), 3, "e4m3")
    down = hq @ mxq(f64(Wd), 1, "e4m3")
    joined = down.transpose(0, 2, 1, 3).reshape(B, S, D)
    return (mxq(joined, 2, "e4m3") @ mxq(f64(Wo), 0, "e4m3")) + f64(x)

@@ -1,0 +1,183 @@
+from contextlib import ExitStack
+
+import concourse.mybir as mybir
+from concourse.masks import make_identity
+
+F32 = mybir.dt.float32
+BF16 = mybir.dt.bfloat16
+U32 = mybir.dt.uint32
+U8 = mybir.dt.uint8
+FP8X4 = mybir.dt.float8_e4m3fn_x4
+
+P = 128
+PACK = 4
+
+BATCH, SEQ, NS, H, DS = 4, 1024, 4, 512, 128
+D = NS * DS
+TOKENS = BATCH * SEQ
+N_TILES = TOKENS // P
+GROUP = 4
+N_GROUPS = N_TILES // GROUP
+AHEAD = 4
+
+FLOPS = 2 * TOKENS * NS * H * DS + 2 * TOKENS * D * D
+
+
+def tile_mopn_layer_pb_t_kernel(tc, hid, Wd, Wo, x, out):
+    nc = tc.nc
+
+    hid_view = hid.rearrange("b s n h -> (b s) (n h)").rearrange("(p j) f -> p j f", j=N_TILES)
+    x_view = x.rearrange("b s d -> (b s) d").rearrange("(p j) d -> p j d", j=N_TILES)
+    out_view = out.rearrange("b s d -> (b s) d").rearrange("(p j) d -> p j d", j=N_TILES)
+
+    with ExitStack() as ctx:
+        ctx.enter_context(tc.manual_schedule())
+        weights = ctx.enter_context(tc.tile_pool(name="weights", bufs=1))
+        hid_pool = ctx.enter_context(tc.tile_pool(name="hid", bufs=AHEAD))
+        x_pool = ctx.enter_context(tc.tile_pool(name="x", bufs=AHEAD))
+        out_pool = ctx.enter_context(tc.tile_pool(name="out", bufs=3))
+        stage = ctx.enter_context(tc.tile_pool(name="stage", bufs=3))
+        psum_turned = ctx.enter_context(tc.psum_pool(name="psum_turned", bufs=4))
+        psum_down = ctx.enter_context(tc.psum_pool(name="psum_down", bufs=2))
+        psum_mixed = ctx.enter_context(tc.psum_pool(name="psum_mixed", bufs=2))
+
+        hid_sb, x_sb, out_sb = {}, {}, {}
+        turned, grouped, h_codes, h_scales = {}, {}, {}, {}
+        down, j_grouped, j_codes, j_scales, mixed = {}, {}, {}, {}, {}
+
+        def load_group(g):
+            tiles = slice(g * GROUP, (g + 1) * GROUP)
+            hid_sb[g] = hid_pool.tile([P, GROUP, NS * H], BF16, name="hid_sb")
+            nc.sync.dma_start(out=hid_sb[g][:], in_=hid_view[:, tiles, :])
+            x_sb[g] = x_pool.tile([P, GROUP, D], BF16, name="x_sb")
+            nc.sync.dma_start(out=x_sb[g][:], in_=x_view[:, tiles, :])
+
+        wd_raw = weights.tile([P, NS, PACK, DS], BF16)
+        nc.sync.dma_start(
+            out=wd_raw[:].rearrange("p n (u e) c -> p (n u) (e c)", u=2),
+            in_=Wd.rearrange("n k c -> (n k) c").rearrange("(m q e) c -> q m (e c)", q=P, e=2),
+        )
+        wo_raw = weights.tile([P, PACK, D], BF16)
+        nc.sync.dma_start(out=wo_raw[:], in_=Wo.rearrange("(t p) c -> p t c", p=P))
+
+        for g in range(AHEAD):
+            load_group(g)
+
+        ident = weights.tile([P, P], F32)
+        make_identity(nc, ident[:])
+
+        wd_grouped = weights.tile([P, NS, DS, PACK], BF16, align_bytes=64)
+        nc.vector.tensor_copy(out=wd_grouped[:], in_=wd_raw[:].rearrange("p n t c -> p n c t"))
+        wo_grouped = weights.tile([P, D, PACK], BF16, align_bytes=64)
+        nc.scalar.copy(out=wo_grouped[:], in_=wo_raw[:].rearrange("p t c -> p c t"))
+        wd_codes = weights.tile([P, NS * DS], U32, align_bytes=64)
+        wd_scales = weights.tile([P, NS * DS], U8, align_bytes=64)
+        nc.vector.quantize_mx(
+            out=wd_codes[:].bitcast(FP8X4),
+            scales=wd_scales[:],
+            in_=wd_grouped[:].rearrange("p n c t -> p (n c t)"),
+        )
+        wo_codes = weights.tile([P, D], U32, align_bytes=64)
+        wo_scales = weights.tile([P, D], U8, align_bytes=64)
+        nc.vector.quantize_mx(
+            out=wo_codes[:].bitcast(FP8X4),
+            scales=wo_scales[:],
+            in_=wo_grouped[:].rearrange("p c t -> p (c t)"),
+        )
+
+        def transpose_hid(i):
+            g, j = divmod(i, GROUP)
+            words = hid_sb[g][:, j, :].bitcast(F32)
+            turned[i] = []
+            for half in range(2):
+                bank = psum_turned.tile([P, 2, 2, P], F32)
+                for nn in range(2):
+                    for u in range(2):
+                        first = ((2 * half + nn) * 2 + u) * P
+                        nc.tensor.transpose(bank[:, nn, u, :], words[:, first : first + P], ident[:])
+                turned[i].append(bank)
+
+        def regroup_hid(i):
+            grouped[i] = stage.tile([P, NS * P * PACK], BF16, align_bytes=64, name="grouped")
+            pairs = grouped[i][:].bitcast(F32).rearrange("p (n r u) -> p n r u", n=NS, u=2)
+            for half in range(2):
+                nc.scalar.copy(
+                    out=pairs[:, 2 * half : 2 * half + 2],
+                    in_=turned[i][half][:].rearrange("p n u r -> p n r u"),
+                )
+
+        def quantise_hid(i):
+            h_codes[i] = stage.tile([P, NS * P], U32, align_bytes=64, name="h_codes")
+            h_scales[i] = stage.tile([P, NS * P], U8, align_bytes=64, name="h_scales")
+            nc.vector.quantize_mx(
+                out=h_codes[i][:].bitcast(FP8X4), scales=h_scales[i][:], in_=grouped[i][:]
+            )
+
+        def project_down(i):
+            down[i] = psum_down.tile([P, NS, P], F32, name="down")
+            for n in range(NS):
+                cols = slice(n * P, (n + 1) * P)
+                nc.tensor.matmul_mx(
+                    out=down[i][:, n, :],
+                    lhsT=wd_codes[:, cols].bitcast(FP8X4),
+                    lhsT_scale=wd_scales[:, cols],
+                    rhs=h_codes[i][:, cols].bitcast(FP8X4),
+                    rhs_scale=h_scales[i][:, cols],
+                    start=True,
+                    stop=True,
+                )
+
+        def regroup_joined(i):
+            j_grouped[i] = stage.tile([P, P, NS], BF16, align_bytes=64, name="j_grouped")
+            nc.scalar.copy(out=j_grouped[i][:], in_=down[i][:].rearrange("p n r -> p r n"))
+
+        def quantise_joined(i):
+            j_codes[i] = stage.tile([P, P], U32, align_bytes=64, name="j_codes")
+            j_scales[i] = stage.tile([P, P], U8, align_bytes=64, name="j_scales")
+            nc.vector.quantize_mx(
+                out=j_codes[i][:].bitcast(FP8X4),
+                scales=j_scales[i][:],
+                in_=j_grouped[i][:].rearrange("p r n -> p (r n)"),
+            )
+
+        def mix_subspaces(i):
+            mixed[i] = psum_mixed.tile([P, D], F32, name="mixed")
+            nc.tensor.matmul_mx(
+                out=mixed[i][:],
+                lhsT=j_codes[i][:].bitcast(FP8X4),
+                lhsT_scale=j_scales[i][:],
+                rhs=wo_codes[:].bitcast(FP8X4),
+                rhs_scale=wo_scales[:],
+                start=True,
+                stop=True,
+            )
+
+        def add_residual(i):
+            g, j = divmod(i, GROUP)
+            if j == 0:
+                out_sb[g] = out_pool.tile([P, GROUP, D], F32, name="out_sb")
+            nc.vector.tensor_tensor(
+                out=out_sb[g][:, j, :], in0=mixed[i][:], in1=x_sb[g][:, j, :], op=mybir.AluOpType.add
+            )
+            if j == GROUP - 1:
+                nc.sync.dma_start(out=out_view[:, g * GROUP : (g + 1) * GROUP, :], in_=out_sb[g][:])
+                if g + AHEAD < N_GROUPS:
+                    load_group(g + AHEAD)
+
+        def in_range(i):
+            return 0 <= i < N_TILES
+
+        for step in range(N_TILES + 4):
+            if in_range(step):
+                transpose_hid(step)
+                regroup_hid(step)
+            if in_range(step - 1):
+                quantise_hid(step - 1)
+            if in_range(step - 2):
+                project_down(step - 2)
+                regroup_joined(step - 2)
+            if in_range(step - 3):
+                quantise_joined(step - 3)
+            if in_range(step - 4):
+                mix_subspaces(step - 4)
+                add_residual(step - 4)

@@ -45,12 +45,19 @@ def tile_mopn_layer_pb_t_kernel(tc, hid, Wd, Wo, x, out):
         turned, grouped, h_codes, h_scales = {}, {}, {}, {}
         down, j_grouped, j_codes, j_scales, mixed = {}, {}, {}, {}, {}
 
+        def pieces(g):
+            size = 1 if g in (0, N_GROUPS - 1) else GROUP
+            return [(j, j + size) for j in range(0, GROUP, size)]
+
         def load_group(g):
-            tiles = slice(g * GROUP, (g + 1) * GROUP)
+            first = g * GROUP
             hid_sb[g] = hid_pool.tile([P, GROUP, NS * H], BF16, name="hid_sb")
-            nc.sync.dma_start(out=hid_sb[g][:], in_=hid_view[:, tiles, :])
+            for j0, j1 in pieces(g):
+                nc.sync.dma_start(
+                    out=hid_sb[g][:, j0:j1, :], in_=hid_view[:, first + j0 : first + j1, :]
+                )
             x_sb[g] = x_pool.tile([P, GROUP, D], BF16, name="x_sb")
-            nc.sync.dma_start(out=x_sb[g][:], in_=x_view[:, tiles, :])
+            nc.sync.dma_start(out=x_sb[g][:], in_=x_view[:, first : first + GROUP, :])
 
         wd_raw = weights.tile([P, NS, PACK, DS], BF16)
         nc.sync.dma_start(
@@ -69,7 +76,7 @@ def tile_mopn_layer_pb_t_kernel(tc, hid, Wd, Wo, x, out):
         wd_grouped = weights.tile([P, NS, DS, PACK], BF16, align_bytes=64)
         nc.vector.tensor_copy(out=wd_grouped[:], in_=wd_raw[:].rearrange("p n t c -> p n c t"))
         wo_grouped = weights.tile([P, D, PACK], BF16, align_bytes=64)
-        nc.scalar.copy(out=wo_grouped[:], in_=wo_raw[:].rearrange("p t c -> p c t"))
+        nc.vector.tensor_copy(out=wo_grouped[:], in_=wo_raw[:].rearrange("p t c -> p c t"))
         wd_codes = weights.tile([P, NS * DS], U32, align_bytes=64)
         wd_scales = weights.tile([P, NS * DS], U8, align_bytes=64)
         nc.vector.quantize_mx(
@@ -159,10 +166,14 @@ def tile_mopn_layer_pb_t_kernel(tc, hid, Wd, Wo, x, out):
             nc.vector.tensor_tensor(
                 out=out_sb[g][:, j, :], in0=mixed[i][:], in1=x_sb[g][:, j, :], op=mybir.AluOpType.add
             )
-            if j == GROUP - 1:
-                nc.sync.dma_start(out=out_view[:, g * GROUP : (g + 1) * GROUP, :], in_=out_sb[g][:])
-                if g + AHEAD < N_GROUPS:
-                    load_group(g + AHEAD)
+            for j0, j1 in pieces(g):
+                if j1 == j + 1:
+                    first = g * GROUP
+                    nc.sync.dma_start(
+                        out=out_view[:, first + j0 : first + j1, :], in_=out_sb[g][:, j0:j1, :]
+                    )
+            if j == GROUP - 1 and g + AHEAD < N_GROUPS:
+                load_group(g + AHEAD)
 
         def in_range(i):
             return 0 <= i < N_TILES

@@ -18,7 +18,8 @@ TOKENS = BATCH * SEQ
 N_TILES = TOKENS // P
 GROUP = 4
 N_GROUPS = N_TILES // GROUP
-AHEAD = 4
+AHEAD = 5
+VECTOR_TURN = 4
 
 FLOPS = 2 * TOKENS * NS * H * DS + 2 * TOKENS * D * D
 
@@ -35,7 +36,7 @@ def tile_mopn_layer_pb_t_kernel(tc, hid, Wd, Wo, x, out):
         weights = ctx.enter_context(tc.tile_pool(name="weights", bufs=1))
         hid_pool = ctx.enter_context(tc.tile_pool(name="hid", bufs=AHEAD))
         x_pool = ctx.enter_context(tc.tile_pool(name="x", bufs=AHEAD))
-        out_pool = ctx.enter_context(tc.tile_pool(name="out", bufs=3))
+        out_pool = ctx.enter_context(tc.tile_pool(name="out", bufs=AHEAD - 1))
         stage = ctx.enter_context(tc.tile_pool(name="stage", bufs=3))
         psum_turned = ctx.enter_context(tc.psum_pool(name="psum_turned", bufs=4))
         psum_down = ctx.enter_context(tc.psum_pool(name="psum_down", bufs=2))
@@ -45,14 +46,14 @@ def tile_mopn_layer_pb_t_kernel(tc, hid, Wd, Wo, x, out):
         turned, grouped, h_codes, h_scales = {}, {}, {}, {}
         down, j_grouped, j_codes, j_scales, mixed = {}, {}, {}, {}, {}
 
-        def pieces(g):
-            size = 1 if g in (0, N_GROUPS - 1) else GROUP
+        def pieces(whole):
+            size = GROUP if whole else 1
             return [(j, j + size) for j in range(0, GROUP, size)]
 
         def load_group(g):
             first = g * GROUP
             hid_sb[g] = hid_pool.tile([P, GROUP, NS * H], BF16, name="hid_sb")
-            for j0, j1 in pieces(g):
+            for j0, j1 in pieces(whole=0 < g < N_GROUPS - 1):
                 nc.sync.dma_start(
                     out=hid_sb[g][:, j0:j1, :], in_=hid_view[:, first + j0 : first + j1, :]
                 )
@@ -136,7 +137,11 @@ def tile_mopn_layer_pb_t_kernel(tc, hid, Wd, Wo, x, out):
 
         def regroup_joined(i):
             j_grouped[i] = stage.tile([P, P, NS], BF16, align_bytes=64, name="j_grouped")
-            nc.scalar.copy(out=j_grouped[i][:], in_=down[i][:].rearrange("p n r -> p r n"))
+            side_by_side = down[i][:].rearrange("p n r -> p r n")
+            if i % VECTOR_TURN == VECTOR_TURN - 1:
+                nc.vector.tensor_copy(out=j_grouped[i][:], in_=side_by_side)
+            else:
+                nc.scalar.copy(out=j_grouped[i][:], in_=side_by_side)
 
         def quantise_joined(i):
             j_codes[i] = stage.tile([P, P], U32, align_bytes=64, name="j_codes")
@@ -166,7 +171,7 @@ def tile_mopn_layer_pb_t_kernel(tc, hid, Wd, Wo, x, out):
             nc.vector.tensor_tensor(
                 out=out_sb[g][:, j, :], in0=mixed[i][:], in1=x_sb[g][:, j, :], op=mybir.AluOpType.add
             )
-            for j0, j1 in pieces(g):
+            for j0, j1 in pieces(whole=g < N_GROUPS - 1):
                 if j1 == j + 1:
                     first = g * GROUP
                     nc.sync.dma_start(
@@ -186,9 +191,10 @@ def tile_mopn_layer_pb_t_kernel(tc, hid, Wd, Wo, x, out):
                 quantise_hid(step - 1)
             if in_range(step - 2):
                 project_down(step - 2)
-                regroup_joined(step - 2)
             if in_range(step - 3):
                 quantise_joined(step - 3)
+            if in_range(step - 2):
+                regroup_joined(step - 2)
             if in_range(step - 4):
                 mix_subspaces(step - 4)
                 add_residual(step - 4)

@@ -18,7 +18,7 @@ TOKENS = BATCH * SEQ
 N_TILES = TOKENS // P
 GROUP = 4
 N_GROUPS = N_TILES // GROUP
-AHEAD = 5
+HID_BUFS = 5
 VECTOR_TURN = 4
 
 FLOPS = 2 * TOKENS * NS * H * DS + 2 * TOKENS * D * D
@@ -34,9 +34,9 @@ def tile_mopn_layer_pb_t_kernel(tc, hid, Wd, Wo, x, out):
     with ExitStack() as ctx:
         ctx.enter_context(tc.manual_schedule())
         weights = ctx.enter_context(tc.tile_pool(name="weights", bufs=1))
-        hid_pool = ctx.enter_context(tc.tile_pool(name="hid", bufs=AHEAD))
-        x_pool = ctx.enter_context(tc.tile_pool(name="x", bufs=AHEAD))
-        out_pool = ctx.enter_context(tc.tile_pool(name="out", bufs=AHEAD - 1))
+        hid_pool = ctx.enter_context(tc.tile_pool(name="hid", bufs=HID_BUFS))
+        x_pool = ctx.enter_context(tc.tile_pool(name="x", bufs=N_GROUPS))
+        out_pool = ctx.enter_context(tc.tile_pool(name="out", bufs=N_GROUPS))
         stage = ctx.enter_context(tc.tile_pool(name="stage", bufs=3))
         psum_turned = ctx.enter_context(tc.psum_pool(name="psum_turned", bufs=4))
         psum_down = ctx.enter_context(tc.psum_pool(name="psum_down", bufs=2))
@@ -68,7 +68,7 @@ def tile_mopn_layer_pb_t_kernel(tc, hid, Wd, Wo, x, out):
         wo_raw = weights.tile([P, PACK, D], BF16)
         nc.sync.dma_start(out=wo_raw[:], in_=Wo.rearrange("(t p) c -> p t c", p=P))
 
-        for g in range(AHEAD):
+        for g in range(HID_BUFS):
             load_group(g)
 
         ident = weights.tile([P, P], F32)
@@ -104,6 +104,8 @@ def tile_mopn_layer_pb_t_kernel(tc, hid, Wd, Wo, x, out):
                         first = ((2 * half + nn) * 2 + u) * P
                         nc.tensor.transpose(bank[:, nn, u, :], words[:, first : first + P], ident[:])
                 turned[i].append(bank)
+            if j == GROUP - 1 and g + HID_BUFS < N_GROUPS:
+                load_group(g + HID_BUFS)
 
         def regroup_hid(i):
             grouped[i] = stage.tile([P, NS * P * PACK], BF16, align_bytes=64, name="grouped")
@@ -171,14 +173,6 @@ def tile_mopn_layer_pb_t_kernel(tc, hid, Wd, Wo, x, out):
             nc.vector.tensor_tensor(
                 out=out_sb[g][:, j, :], in0=mixed[i][:], in1=x_sb[g][:, j, :], op=mybir.AluOpType.add
             )
-            for j0, j1 in pieces(whole=g < N_GROUPS - 1):
-                if j1 == j + 1:
-                    first = g * GROUP
-                    nc.sync.dma_start(
-                        out=out_view[:, first + j0 : first + j1, :], in_=out_sb[g][:, j0:j1, :]
-                    )
-            if j == GROUP - 1 and g + AHEAD < N_GROUPS:
-                load_group(g + AHEAD)
 
         def in_range(i):
             return 0 <= i < N_TILES
@@ -198,3 +192,10 @@ def tile_mopn_layer_pb_t_kernel(tc, hid, Wd, Wo, x, out):
             if in_range(step - 4):
                 mix_subspaces(step - 4)
                 add_residual(step - 4)
+
+        for g in range(N_GROUPS):
+            first = g * GROUP
+            for j0, j1 in pieces(whole=g < N_GROUPS - 1):
+                nc.sync.dma_start(
+                    out=out_view[:, first + j0 : first + j1, :], in_=out_sb[g][:, j0:j1, :]
+                )

@@ -19,6 +19,8 @@ N_TILES = TOKENS // P
 GROUP = 4
 N_GROUPS = N_TILES // GROUP
 HID_BUFS = 5
+X_GROUPS = 4
+STORE_TILES = (8, 8, 8, 4, 1, 1, 1, 1)
 VECTOR_TURN = 4
 
 FLOPS = 2 * TOKENS * NS * H * DS + 2 * TOKENS * D * D
@@ -35,14 +37,13 @@ def tile_mopn_layer_pb_t_kernel(tc, hid, Wd, Wo, x, out):
         ctx.enter_context(tc.manual_schedule())
         weights = ctx.enter_context(tc.tile_pool(name="weights", bufs=1))
         hid_pool = ctx.enter_context(tc.tile_pool(name="hid", bufs=HID_BUFS))
-        x_pool = ctx.enter_context(tc.tile_pool(name="x", bufs=N_GROUPS))
-        out_pool = ctx.enter_context(tc.tile_pool(name="out", bufs=N_GROUPS))
+        whole = ctx.enter_context(tc.tile_pool(name="whole", bufs=1))
         stage = ctx.enter_context(tc.tile_pool(name="stage", bufs=3))
         psum_turned = ctx.enter_context(tc.psum_pool(name="psum_turned", bufs=4))
         psum_down = ctx.enter_context(tc.psum_pool(name="psum_down", bufs=2))
         psum_mixed = ctx.enter_context(tc.psum_pool(name="psum_mixed", bufs=2))
 
-        hid_sb, x_sb, out_sb = {}, {}, {}
+        hid_sb = {}
         turned, grouped, h_codes, h_scales = {}, {}, {}, {}
         down, j_grouped, j_codes, j_scales, mixed = {}, {}, {}, {}, {}
 
@@ -57,8 +58,14 @@ def tile_mopn_layer_pb_t_kernel(tc, hid, Wd, Wo, x, out):
                 nc.sync.dma_start(
                     out=hid_sb[g][:, j0:j1, :], in_=hid_view[:, first + j0 : first + j1, :]
                 )
-            x_sb[g] = x_pool.tile([P, GROUP, D], BF16, name="x_sb")
-            nc.sync.dma_start(out=x_sb[g][:], in_=x_view[:, first : first + GROUP, :])
+            if g % X_GROUPS == 0:
+                load_x(first, first + X_GROUPS * GROUP)
+
+        x_sb = whole.tile([P, N_TILES, D], BF16)
+        out_sb = whole.tile([P, N_TILES, D], F32)
+
+        def load_x(first, last):
+            nc.sync.dma_start(out=x_sb[:, first:last, :], in_=x_view[:, first:last, :])
 
         wd_raw = weights.tile([P, NS, PACK, DS], BF16)
         nc.sync.dma_start(
@@ -167,11 +174,8 @@ def tile_mopn_layer_pb_t_kernel(tc, hid, Wd, Wo, x, out):
             )
 
         def add_residual(i):
-            g, j = divmod(i, GROUP)
-            if j == 0:
-                out_sb[g] = out_pool.tile([P, GROUP, D], F32, name="out_sb")
             nc.vector.tensor_tensor(
-                out=out_sb[g][:, j, :], in0=mixed[i][:], in1=x_sb[g][:, j, :], op=mybir.AluOpType.add
+                out=out_sb[:, i, :], in0=mixed[i][:], in1=x_sb[:, i, :], op=mybir.AluOpType.add
             )
 
         def in_range(i):
@@ -193,9 +197,9 @@ def tile_mopn_layer_pb_t_kernel(tc, hid, Wd, Wo, x, out):
                 mix_subspaces(step - 4)
                 add_residual(step - 4)
 
-        for g in range(N_GROUPS):
-            first = g * GROUP
-            for j0, j1 in pieces(whole=g < N_GROUPS - 1):
-                nc.sync.dma_start(
-                    out=out_view[:, first + j0 : first + j1, :], in_=out_sb[g][:, j0:j1, :]
-                )
+        first = 0
+        for tiles in STORE_TILES:
+            nc.sync.dma_start(
+                out=out_view[:, first : first + tiles, :], in_=out_sb[:, first : first + tiles, :]
+            )
+            first += tiles

@@ -19,8 +19,7 @@ N_TILES = TOKENS // P
 GROUP = 4
 N_GROUPS = N_TILES // GROUP
 HID_BUFS = 5
-X_GROUPS = 4
-STORE_TILES = (8, 8, 8, 4, 1, 1, 1, 1)
+STORE_TILES = (8, 8, 8, 4, 2, 1, 1)
 VECTOR_TURN = 4
 
 FLOPS = 2 * TOKENS * NS * H * DS + 2 * TOKENS * D * D
@@ -44,61 +43,75 @@ def tile_mopn_layer_pb_t_kernel(tc, hid, Wd, Wo, x, out):
         psum_mixed = ctx.enter_context(tc.psum_pool(name="psum_mixed", bufs=2))
 
         hid_sb = {}
+        x_sb = whole.tile([P, N_TILES, D], BF16)
+        out_sb = whole.tile([P, N_TILES, D], F32)
         turned, grouped, h_codes, h_scales = {}, {}, {}, {}
         down, j_grouped, j_codes, j_scales, mixed = {}, {}, {}, {}, {}
 
-        def pieces(whole):
-            size = GROUP if whole else 1
-            return [(j, j + size) for j in range(0, GROUP, size)]
-
-        def load_group(g):
-            first = g * GROUP
-            hid_sb[g] = hid_pool.tile([P, GROUP, NS * H], BF16, name="hid_sb")
-            for j0, j1 in pieces(whole=0 < g < N_GROUPS - 1):
-                nc.sync.dma_start(
-                    out=hid_sb[g][:, j0:j1, :], in_=hid_view[:, first + j0 : first + j1, :]
-                )
-            if g % X_GROUPS == 0:
-                load_x(first, first + X_GROUPS * GROUP)
-
-        x_sb = whole.tile([P, N_TILES, D], BF16)
-        out_sb = whole.tile([P, N_TILES, D], F32)
+        def load_hid(first, last):
+            g, j0 = divmod(first, GROUP)
+            if j0 == 0:
+                hid_sb[g] = hid_pool.tile([P, GROUP, NS * H], BF16, name="hid_sb")
+            nc.sync.dma_start(
+                out=hid_sb[g][:, j0 : j0 + last - first, :], in_=hid_view[:, first:last, :]
+            )
 
         def load_x(first, last):
             nc.sync.dma_start(out=x_sb[:, first:last, :], in_=x_view[:, first:last, :])
 
         wd_raw = weights.tile([P, NS, PACK, DS], BF16)
-        nc.sync.dma_start(
-            out=wd_raw[:].rearrange("p n (u e) c -> p (n u) (e c)", u=2),
-            in_=Wd.rearrange("n k c -> (n k) c").rearrange("(m q e) c -> q m (e c)", q=P, e=2),
-        )
-        wo_raw = weights.tile([P, PACK, D], BF16)
-        nc.sync.dma_start(out=wo_raw[:], in_=Wo.rearrange("(t p) c -> p t c", p=P))
 
-        for g in range(HID_BUFS):
-            load_group(g)
+        def load_wd():
+            nc.sync.dma_start(
+                out=wd_raw[:].rearrange("p n (u e) c -> p (n u) (e c)", u=2),
+                in_=Wd.rearrange("n k c -> (n k) c").rearrange("(m q e) c -> q m (e c)", q=P, e=2),
+            )
+
+        wo_raw = weights.tile([P, PACK, D], BF16)
+
+        def load_wo():
+            nc.sync.dma_start(out=wo_raw[:], in_=Wo.rearrange("(t p) c -> p t c", p=P))
+
+        load_hid(0, 1)
+        load_wd()
+        load_hid(1, 2)
+        load_wo()
+        load_hid(2, 4)
+        load_hid(4, 6)
+        load_x(0, 8)
+        load_hid(6, 8)
+        load_hid(8, 12)
+        load_hid(12, 16)
+        load_x(8, 16)
+        load_hid(16, 20)
 
         ident = weights.tile([P, P], F32)
         make_identity(nc, ident[:])
 
         wd_grouped = weights.tile([P, NS, DS, PACK], BF16, align_bytes=64)
-        nc.vector.tensor_copy(out=wd_grouped[:], in_=wd_raw[:].rearrange("p n t c -> p n c t"))
         wo_grouped = weights.tile([P, D, PACK], BF16, align_bytes=64)
-        nc.vector.tensor_copy(out=wo_grouped[:], in_=wo_raw[:].rearrange("p t c -> p c t"))
         wd_codes = weights.tile([P, NS * DS], U32, align_bytes=64)
         wd_scales = weights.tile([P, NS * DS], U8, align_bytes=64)
-        nc.vector.quantize_mx(
-            out=wd_codes[:].bitcast(FP8X4),
-            scales=wd_scales[:],
-            in_=wd_grouped[:].rearrange("p n c t -> p (n c t)"),
-        )
         wo_codes = weights.tile([P, D], U32, align_bytes=64)
         wo_scales = weights.tile([P, D], U8, align_bytes=64)
-        nc.vector.quantize_mx(
-            out=wo_codes[:].bitcast(FP8X4),
-            scales=wo_scales[:],
-            in_=wo_grouped[:].rearrange("p c t -> p (c t)"),
-        )
+
+        def prepare_wd():
+            nc.vector.tensor_copy(
+                out=wd_grouped[:], in_=wd_raw[:].rearrange("p n t c -> p n c t")
+            )
+            nc.vector.quantize_mx(
+                out=wd_codes[:].bitcast(FP8X4),
+                scales=wd_scales[:],
+                in_=wd_grouped[:].rearrange("p n c t -> p (n c t)"),
+            )
+
+        def prepare_wo():
+            nc.vector.tensor_copy(out=wo_grouped[:], in_=wo_raw[:].rearrange("p t c -> p c t"))
+            nc.vector.quantize_mx(
+                out=wo_codes[:].bitcast(FP8X4),
+                scales=wo_scales[:],
+                in_=wo_grouped[:].rearrange("p c t -> p (c t)"),
+            )
 
         def transpose_hid(i):
             g, j = divmod(i, GROUP)
@@ -112,7 +125,10 @@ def tile_mopn_layer_pb_t_kernel(tc, hid, Wd, Wo, x, out):
                         nc.tensor.transpose(bank[:, nn, u, :], words[:, first : first + P], ident[:])
                 turned[i].append(bank)
             if j == GROUP - 1 and g + HID_BUFS < N_GROUPS:
-                load_group(g + HID_BUFS)
+                later = (g + HID_BUFS) * GROUP
+                load_hid(later, later + GROUP)
+                if g == 0:
+                    load_x(16, N_TILES)
 
         def regroup_hid(i):
             grouped[i] = stage.tile([P, NS * P * PACK], BF16, align_bytes=64, name="grouped")
@@ -187,10 +203,14 @@ def tile_mopn_layer_pb_t_kernel(tc, hid, Wd, Wo, x, out):
                 regroup_hid(step)
             if in_range(step - 1):
                 quantise_hid(step - 1)
+            if step == 1:
+                prepare_wd()
             if in_range(step - 2):
                 project_down(step - 2)
             if in_range(step - 3):
                 quantise_joined(step - 3)
+            if step == 3:
+                prepare_wo()
             if in_range(step - 2):
                 regroup_joined(step - 2)
             if in_range(step - 4):

@@ -59,18 +59,17 @@ def tile_mopn_layer_pb_t_kernel(tc, hid, Wd, Wo, x, out):
         def load_x(first, last):
             nc.sync.dma_start(out=x_sb[:, first:last, :], in_=x_view[:, first:last, :])
 
-        wd_raw = weights.tile([P, NS, PACK, DS], BF16)
+        wd_raw = weights.tile([P, 16 * DS], BF16)
+        wo_raw = weights.tile([P, PACK * D], BF16)
 
         def load_wd():
             nc.sync.dma_start(
-                out=wd_raw[:].rearrange("p n (u e) c -> p (n u) (e c)", u=2),
-                in_=Wd.rearrange("n k c -> (n k) c").rearrange("(m q e) c -> q m (e c)", q=P, e=2),
+                out=wd_raw[:],
+                in_=Wd.rearrange("n k c -> (n k) c").rearrange("(q r) c -> q (r c)", q=P),
             )
 
-        wo_raw = weights.tile([P, PACK, D], BF16)
-
         def load_wo():
-            nc.sync.dma_start(out=wo_raw[:], in_=Wo.rearrange("(t p) c -> p t c", p=P))
+            nc.sync.dma_start(out=wo_raw[:], in_=Wo.rearrange("(q r) c -> q (r c)", q=P))
 
         load_hid(0, 1)
         load_wd()
@@ -95,18 +94,62 @@ def tile_mopn_layer_pb_t_kernel(tc, hid, Wd, Wo, x, out):
         wo_codes = weights.tile([P, D], U32, align_bytes=64)
         wo_scales = weights.tile([P, D], U8, align_bytes=64)
 
+        wd_columns = weights.tile([P, P, 8], F32)
+        wo_columns = weights.tile([P, 2, P, PACK], F32)
+
+        def four_transposes(blocks):
+            bank = psum_turned.tile([P, 2, 2, P], F32, name="bank")
+            quarters = bank[:].rearrange("p a b c -> p (a b) c")
+            for place, block in enumerate(blocks):
+                nc.tensor.transpose(quarters[:, place, :], block, ident[:])
+            return quarters
+
+        def block_of(words, index):
+            return words[:, index * P : (index + 1) * P]
+
+        def turn_wd():
+            words = wd_raw[:].bitcast(F32)
+            for half in range(2):
+                turned_rows = four_transposes([block_of(words, 4 * half + a) for a in range(4)])
+                nc.scalar.copy(
+                    out=wd_columns[:, :, 4 * half : 4 * half + 4],
+                    in_=turned_rows.rearrange("p a q -> p q a"),
+                )
+
         def prepare_wd():
-            nc.vector.tensor_copy(
-                out=wd_grouped[:], in_=wd_raw[:].rearrange("p n t c -> p n c t")
-            )
+            columns = wd_columns[:].rearrange("p q a -> p (q a)")
+            for half in range(2):
+                rows = four_transposes([block_of(columns, 4 * half + m) for m in range(4)])
+                nc.vector.tensor_copy(
+                    out=wd_grouped[:, 2 * half : 2 * half + 2],
+                    in_=rows.rearrange("p m w -> p (m w)")
+                    .bitcast(BF16)
+                    .rearrange("p (n t c) -> p n c t", n=2, t=PACK),
+                )
             nc.vector.quantize_mx(
                 out=wd_codes[:].bitcast(FP8X4),
                 scales=wd_scales[:],
                 in_=wd_grouped[:].rearrange("p n c t -> p (n c t)"),
             )
 
+        def turn_wo():
+            words = wo_raw[:].bitcast(F32)
+            for half in range(2):
+                turned_rows = four_transposes([block_of(words, 2 * r + half) for r in range(PACK)])
+                nc.scalar.copy(
+                    out=wo_columns[:, half], in_=turned_rows.rearrange("p r q -> p q r")
+                )
+
         def prepare_wo():
-            nc.vector.tensor_copy(out=wo_grouped[:], in_=wo_raw[:].rearrange("p t c -> p c t"))
+            for half in range(2):
+                columns = wo_columns[:, half].rearrange("p q r -> p (q r)")
+                rows = four_transposes([block_of(columns, t) for t in range(PACK)])
+                nc.vector.tensor_copy(
+                    out=wo_grouped[:, half * 2 * P : (half + 1) * 2 * P],
+                    in_=rows.rearrange("p t w -> p (t w)")
+                    .bitcast(BF16)
+                    .rearrange("p (t c) -> p c t", t=PACK),
+                )
             nc.vector.quantize_mx(
                 out=wo_codes[:].bitcast(FP8X4),
                 scales=wo_scales[:],
@@ -118,7 +161,7 @@ def tile_mopn_layer_pb_t_kernel(tc, hid, Wd, Wo, x, out):
             words = hid_sb[g][:, j, :].bitcast(F32)
             turned[i] = []
             for half in range(2):
-                bank = psum_turned.tile([P, 2, 2, P], F32)
+                bank = psum_turned.tile([P, 2, 2, P], F32, name="bank")
                 for nn in range(2):
                     for u in range(2):
                         first = ((2 * half + nn) * 2 + u) * P
@@ -201,6 +244,10 @@ def tile_mopn_layer_pb_t_kernel(tc, hid, Wd, Wo, x, out):
             if in_range(step):
                 transpose_hid(step)
                 regroup_hid(step)
+            if step == 0:
+                turn_wd()
+            if step == 2:
+                turn_wo()
             if in_range(step - 1):
                 quantise_hid(step - 1)
             if step == 1:

@@ -71,14 +71,12 @@ def tile_mopn_layer_pb_t_kernel(tc, hid, Wd, Wo, x, out):
         def load_wo():
             nc.sync.dma_start(out=wo_raw[:], in_=Wo.rearrange("(q r) c -> q (r c)", q=P))
 
-        load_hid(0, 1)
         load_wd()
-        load_hid(1, 2)
+        load_hid(0, 2)
         load_wo()
         load_hid(2, 4)
-        load_hid(4, 6)
+        load_hid(4, 8)
         load_x(0, 8)
-        load_hid(6, 8)
         load_hid(8, 12)
         load_hid(12, 16)
         load_x(8, 16)
@@ -240,23 +238,22 @@ def tile_mopn_layer_pb_t_kernel(tc, hid, Wd, Wo, x, out):
         def in_range(i):
             return 0 <= i < N_TILES
 
+        turn_wd()
         for step in range(N_TILES + 4):
             if in_range(step):
                 transpose_hid(step)
                 regroup_hid(step)
             if step == 0:
-                turn_wd()
-            if step == 2:
+                prepare_wd()
+            if step == 1:
                 turn_wo()
             if in_range(step - 1):
                 quantise_hid(step - 1)
-            if step == 1:
-                prepare_wd()
             if in_range(step - 2):
                 project_down(step - 2)
             if in_range(step - 3):
                 quantise_joined(step - 3)
-            if step == 3:
+            if step == 2:
                 prepare_wo()
             if in_range(step - 2):
                 regroup_joined(step - 2)

from contextlib import ExitStack

import concourse.mybir as mybir
from concourse.masks import make_identity

F32 = mybir.dt.float32
BF16 = mybir.dt.bfloat16
U32 = mybir.dt.uint32
U8 = mybir.dt.uint8
FP8X4 = mybir.dt.float8_e4m3fn_x4

P = 128
PACK = 4

BATCH, SEQ, NS, H, DS = 4, 1024, 4, 512, 128
D = NS * DS
TOKENS = BATCH * SEQ
N_TILES = TOKENS // P
GROUP = 4
N_GROUPS = N_TILES // GROUP
HID_BUFS = 5
STORE_TILES = (8, 8, 8, 4, 2, 1, 1)
VECTOR_TURN = 4

FLOPS = 2 * TOKENS * NS * H * DS + 2 * TOKENS * D * D


def tile_mopn_layer_pb_t_kernel(tc, hid, Wd, Wo, x, out):
    nc = tc.nc

    hid_view = hid.rearrange("b s n h -> (b s) (n h)").rearrange("(p j) f -> p j f", j=N_TILES)
    x_view = x.rearrange("b s d -> (b s) d").rearrange("(p j) d -> p j d", j=N_TILES)
    out_view = out.rearrange("b s d -> (b s) d").rearrange("(p j) d -> p j d", j=N_TILES)

    with ExitStack() as ctx:
        ctx.enter_context(tc.manual_schedule())
        weights = ctx.enter_context(tc.tile_pool(name="weights", bufs=1))
        hid_pool = ctx.enter_context(tc.tile_pool(name="hid", bufs=HID_BUFS))
        whole = ctx.enter_context(tc.tile_pool(name="whole", bufs=1))
        stage = ctx.enter_context(tc.tile_pool(name="stage", bufs=3))
        psum_turned = ctx.enter_context(tc.psum_pool(name="psum_turned", bufs=4))
        psum_down = ctx.enter_context(tc.psum_pool(name="psum_down", bufs=2))
        psum_mixed = ctx.enter_context(tc.psum_pool(name="psum_mixed", bufs=2))

        hid_sb = {}
        x_sb = whole.tile([P, N_TILES, D], BF16)
        out_sb = whole.tile([P, N_TILES, D], F32)
        turned, grouped, h_codes, h_scales = {}, {}, {}, {}
        down, j_grouped, j_codes, j_scales, mixed = {}, {}, {}, {}, {}

        def load_hid(first, last):
            g, j0 = divmod(first, GROUP)
            if j0 == 0:
                hid_sb[g] = hid_pool.tile([P, GROUP, NS * H], BF16, name="hid_sb")
            nc.sync.dma_start(
                out=hid_sb[g][:, j0 : j0 + last - first, :], in_=hid_view[:, first:last, :]
            )

        def load_x(first, last):
            nc.sync.dma_start(out=x_sb[:, first:last, :], in_=x_view[:, first:last, :])

        wd_raw = weights.tile([P, 16 * DS], BF16)
        wo_raw = weights.tile([P, PACK * D], BF16)

        def load_wd():
            nc.sync.dma_start(
                out=wd_raw[:],
                in_=Wd.rearrange("n k c -> (n k) c").rearrange("(q r) c -> q (r c)", q=P),
            )

        def load_wo():
            nc.sync.dma_start(out=wo_raw[:], in_=Wo.rearrange("(q r) c -> q (r c)", q=P))

        load_wd()
        load_hid(0, 2)
        load_wo()
        load_hid(2, 4)
        load_hid(4, 8)
        load_x(0, 8)
        load_hid(8, 12)
        load_hid(12, 16)
        load_x(8, 16)
        load_hid(16, 20)

        ident = weights.tile([P, P], F32)
        make_identity(nc, ident[:])

        wd_grouped = weights.tile([P, NS, DS, PACK], BF16, align_bytes=64)
        wo_grouped = weights.tile([P, D, PACK], BF16, align_bytes=64)
        wd_codes = weights.tile([P, NS * DS], U32, align_bytes=64)
        wd_scales = weights.tile([P, NS * DS], U8, align_bytes=64)
        wo_codes = weights.tile([P, D], U32, align_bytes=64)
        wo_scales = weights.tile([P, D], U8, align_bytes=64)

        wd_columns = weights.tile([P, P, 8], F32)
        wo_columns = weights.tile([P, 2, P, PACK], F32)

        def four_transposes(blocks):
            bank = psum_turned.tile([P, 2, 2, P], F32, name="bank")
            quarters = bank[:].rearrange("p a b c -> p (a b) c")
            for place, block in enumerate(blocks):
                nc.tensor.transpose(quarters[:, place, :], block, ident[:])
            return quarters

        def block_of(words, index):
            return words[:, index * P : (index + 1) * P]

        def turn_wd():
            words = wd_raw[:].bitcast(F32)
            for half in range(2):
                turned_rows = four_transposes([block_of(words, 4 * half + a) for a in range(4)])
                nc.scalar.copy(
                    out=wd_columns[:, :, 4 * half : 4 * half + 4],
                    in_=turned_rows.rearrange("p a q -> p q a"),
                )

        def prepare_wd():
            columns = wd_columns[:].rearrange("p q a -> p (q a)")
            for half in range(2):
                rows = four_transposes([block_of(columns, 4 * half + m) for m in range(4)])
                nc.vector.tensor_copy(
                    out=wd_grouped[:, 2 * half : 2 * half + 2],
                    in_=rows.rearrange("p m w -> p (m w)")
                    .bitcast(BF16)
                    .rearrange("p (n t c) -> p n c t", n=2, t=PACK),
                )
            nc.vector.quantize_mx(
                out=wd_codes[:].bitcast(FP8X4),
                scales=wd_scales[:],
                in_=wd_grouped[:].rearrange("p n c t -> p (n c t)"),
            )

        def turn_wo():
            words = wo_raw[:].bitcast(F32)
            for half in range(2):
                turned_rows = four_transposes([block_of(words, 2 * r + half) for r in range(PACK)])
                nc.scalar.copy(
                    out=wo_columns[:, half], in_=turned_rows.rearrange("p r q -> p q r")
                )

        def prepare_wo():
            for half in range(2):
                columns = wo_columns[:, half].rearrange("p q r -> p (q r)")
                rows = four_transposes([block_of(columns, t) for t in range(PACK)])
                nc.vector.tensor_copy(
                    out=wo_grouped[:, half * 2 * P : (half + 1) * 2 * P],
                    in_=rows.rearrange("p t w -> p (t w)")
                    .bitcast(BF16)
                    .rearrange("p (t c) -> p c t", t=PACK),
                )
            nc.vector.quantize_mx(
                out=wo_codes[:].bitcast(FP8X4),
                scales=wo_scales[:],
                in_=wo_grouped[:].rearrange("p c t -> p (c t)"),
            )

        def transpose_hid(i):
            g, j = divmod(i, GROUP)
            words = hid_sb[g][:, j, :].bitcast(F32)
            turned[i] = []
            for half in range(2):
                bank = psum_turned.tile([P, 2, 2, P], F32, name="bank")
                for nn in range(2):
                    for u in range(2):
                        first = ((2 * half + nn) * 2 + u) * P
                        nc.tensor.transpose(bank[:, nn, u, :], words[:, first : first + P], ident[:])
                turned[i].append(bank)
            if j == GROUP - 1 and g + HID_BUFS < N_GROUPS:
                later = (g + HID_BUFS) * GROUP
                load_hid(later, later + GROUP)
                if g == 0:
                    load_x(16, N_TILES)

        def regroup_hid(i):
            grouped[i] = stage.tile([P, NS * P * PACK], BF16, align_bytes=64, name="grouped")
            pairs = grouped[i][:].bitcast(F32).rearrange("p (n r u) -> p n r u", n=NS, u=2)
            for half in range(2):
                nc.scalar.copy(
                    out=pairs[:, 2 * half : 2 * half + 2],
                    in_=turned[i][half][:].rearrange("p n u r -> p n r u"),
                )

        def quantise_hid(i):
            h_codes[i] = stage.tile([P, NS * P], U32, align_bytes=64, name="h_codes")
            h_scales[i] = stage.tile([P, NS * P], U8, align_bytes=64, name="h_scales")
            nc.vector.quantize_mx(
                out=h_codes[i][:].bitcast(FP8X4), scales=h_scales[i][:], in_=grouped[i][:]
            )

        def project_down(i):
            down[i] = psum_down.tile([P, NS, P], F32, name="down")
            for n in range(NS):
                cols = slice(n * P, (n + 1) * P)
                nc.tensor.matmul_mx(
                    out=down[i][:, n, :],
                    lhsT=wd_codes[:, cols].bitcast(FP8X4),
                    lhsT_scale=wd_scales[:, cols],
                    rhs=h_codes[i][:, cols].bitcast(FP8X4),
                    rhs_scale=h_scales[i][:, cols],
                    start=True,
                    stop=True,
                )

        def regroup_joined(i):
            j_grouped[i] = stage.tile([P, P, NS], BF16, align_bytes=64, name="j_grouped")
            side_by_side = down[i][:].rearrange("p n r -> p r n")
            if i % VECTOR_TURN == VECTOR_TURN - 1:
                nc.vector.tensor_copy(out=j_grouped[i][:], in_=side_by_side)
            else:
                nc.scalar.copy(out=j_grouped[i][:], in_=side_by_side)

        def quantise_joined(i):
            j_codes[i] = stage.tile([P, P], U32, align_bytes=64, name="j_codes")
            j_scales[i] = stage.tile([P, P], U8, align_bytes=64, name="j_scales")
            nc.vector.quantize_mx(
                out=j_codes[i][:].bitcast(FP8X4),
                scales=j_scales[i][:],
                in_=j_grouped[i][:].rearrange("p r n -> p (r n)"),
            )

        def mix_subspaces(i):
            mixed[i] = psum_mixed.tile([P, D], F32, name="mixed")
            nc.tensor.matmul_mx(
                out=mixed[i][:],
                lhsT=j_codes[i][:].bitcast(FP8X4),
                lhsT_scale=j_scales[i][:],
                rhs=wo_codes[:].bitcast(FP8X4),
                rhs_scale=wo_scales[:],
                start=True,
                stop=True,
            )

        def add_residual(i):
            nc.vector.tensor_tensor(
                out=out_sb[:, i, :], in0=mixed[i][:], in1=x_sb[:, i, :], op=mybir.AluOpType.add
            )

        def in_range(i):
            return 0 <= i < N_TILES

        turn_wd()
        for step in range(N_TILES + 4):
            if in_range(step):
                transpose_hid(step)
                regroup_hid(step)
            if step == 0:
                prepare_wd()
            if step == 1:
                turn_wo()
            if in_range(step - 1):
                quantise_hid(step - 1)
            if in_range(step - 2):
                project_down(step - 2)
            if in_range(step - 3):
                quantise_joined(step - 3)
            if step == 2:
                prepare_wo()
            if in_range(step - 2):
                regroup_joined(step - 2)
            if in_range(step - 4):
                mix_subspaces(step - 4)
                add_residual(step - 4)

        first = 0
        for tiles in STORE_TILES:
            nc.sync.dma_start(
                out=out_view[:, first : first + tiles, :], in_=out_sb[:, first : first + tiles, :]
            )
            first += tiles
